import numpy as np
import ml_dtypes


def mxq(x, axis, fmt="e4m3"):
    dtype, down = {"e4m3": (ml_dtypes.float8_e4m3fn, 7), "e5m2": (ml_dtypes.float8_e5m2, 14)}[fmt]
    v = np.moveaxis(np.asarray(x, np.float32).astype(ml_dtypes.bfloat16).astype(np.float64), axis, -1)
    blocks = v.reshape(v.shape[:-1] + (-1, 32))
    amax = np.abs(blocks).max(-1, keepdims=True)
    byte = np.maximum(np.where(amax > 0, np.frexp(amax)[1] - 1 + 127, 0) - down, 1)
    scale = np.exp2(byte - 127.0)
    codes = (blocks / scale).astype(np.float32).astype(dtype).astype(np.float64)
    return np.moveaxis((codes * scale).reshape(v.shape), -1, axis)


WIDE = False


def mx_kscale(k):
    if not WIDE:
        return np.ones(k)
    levels = np.array([10, -10, 5, -5, 0])
    a = np.random.permutation(np.resize(levels, k // 512 * 4)).reshape(k // 512, 4)
    idx = np.arange(k)
    return np.exp2(a[idx // 512, idx % 128 // 32])


BF16 = ml_dtypes.bfloat16


def bf(x):
    return np.asarray(x, np.float32).astype(BF16)


def f64(x):
    return np.asarray(x).astype(np.float64)


B, L, D, H, P, W = 2, 2048, 512, 4, 128, 128
HD = D // H
LT = L + P


def rotate_half(t):
    h = t.shape[-1] // 2
    return np.concatenate([-t[..., h:], t[..., :h]], axis=-1)


def project(pq, xq, w):
    wm = mxq(f64(w), 0, "e4m3")
    tp = pq @ wm
    tx = xq @ wm
    return np.concatenate([np.broadcast_to(tp, (B, P, D)), tx], axis=1).reshape(B, LT, H, HD)


def setup_inputs():
    s = mx_kscale(D)
    return {"x": bf(np.random.standard_normal((B, L, D)) * s),
            "pmem": bf(np.random.standard_normal((1, P, D)) * s),
            "cos": bf(np.random.uniform(size=(LT, HD))),
            "sin": bf(np.random.uniform(size=(LT, HD))),
            "wq": bf(np.random.standard_normal((D, D)) / np.sqrt(D) / s[:, None]),
            "wk": bf(np.random.standard_normal((D, D)) / np.sqrt(D) / s[:, None]),
            "wv": bf(np.random.standard_normal((D, D)) / np.sqrt(D) / s[:, None])}


def reference(x, pmem, cos, sin, wq, wk, wv):
    pq = mxq(f64(pmem), 2, "e4m3")
    xq = mxq(f64(x), 2, "e4m3")
    q = project(pq, xq, wq)
    k = project(pq, xq, wk)
    v = project(pq, xq, wv)
    cc = f64(cos)[None, :, None, :]
    ss = f64(sin)[None, :, None, :]
    q = q * cc + rotate_half(q) * ss
    k = k * cc + rotate_half(k) * ss
    return q, k, v

@@ -1,0 +1,250 @@
+from contextlib import ExitStack
+
+import concourse.mybir as mybir
+from concourse.masks import make_identity
+
+F32 = mybir.dt.float32
+BF16 = mybir.dt.bfloat16
+U32 = mybir.dt.uint32
+U8 = mybir.dt.uint8
+FP8X4 = mybir.dt.float8_e4m3fn_x4
+MULT = mybir.AluOpType.mult
+ADD = mybir.AluOpType.add
+
+P = 128
+PACK = 4
+B = 2
+L = 2048
+D = 512
+H = 4
+HD = D // H
+HALF = HD // 2
+GROUP = 4
+GROUP_TOKENS = GROUP * P
+GROUPS_PER_SEQ = L // GROUP_TOKENS
+TABLE_SLOTS = GROUPS_PER_SEQ * GROUP + 1
+TOKEN_TILES = B * GROUPS_PER_SEQ * GROUP + 1
+WORDS = D // 2
+ADD_TILES = 2
+FIRST = 0
+SECOND = 1
+V = 2
+BANK_TAGS = ("first", "second", "v")
+
+FLOPS = 2 * B * (L + P) * D * 3 * D
+
+
+def token_groups(x, pmem):
+    groups = []
+    for b in range(B):
+        for g in range(GROUPS_PER_SEQ):
+            row = g * GROUP_TOKENS
+            groups.append(
+                {
+                    "rows": x[b, row : row + GROUP_TOKENS, :],
+                    "tiles": GROUP,
+                    "slot": g * GROUP,
+                    "table_row": P + row,
+                    "loads_tables": b == 0,
+                    "stores": [(b, P + row)],
+                }
+            )
+    groups.append(
+        {
+            "rows": pmem[0],
+            "tiles": 1,
+            "slot": GROUPS_PER_SEQ * GROUP,
+            "table_row": 0,
+            "loads_tables": True,
+            "stores": [(b, 0) for b in range(B)],
+        }
+    )
+    first_tile = 0
+    for group in groups:
+        group["first_tile"] = first_tile
+        first_tile += group["tiles"]
+    return groups
+
+
+def tile_titanstnt_pa_t_kernel(tc, x, pmem, cos, sin, wq, wk, wv, out_0, out_1, out_2):
+    nc = tc.nc
+    groups = token_groups(x, pmem)
+
+    with ExitStack() as ctx:
+        keep = ctx.enter_context(tc.tile_pool(name="keep", bufs=1))
+        stage = ctx.enter_context(tc.tile_pool(name="stage", bufs=2))
+        results = ctx.enter_context(tc.tile_pool(name="results", bufs=3))
+        psum = ctx.enter_context(tc.psum_pool(name="psum", bufs=2))
+        ctx.enter_context(tc.manual_schedule())
+
+        x_all = keep.tile([P, TOKEN_TILES * D], BF16)
+        x_words = x_all[:].bitcast(F32)
+        cos_sb = keep.tile([P, TABLE_SLOTS, HD], BF16)
+        sin_sb = keep.tile([P, TABLE_SLOTS, HD], BF16)
+        w_raw = keep.tile([P, 3, PACK, D], BF16)
+        w_grouped = keep.tile([P, 3, D, PACK], BF16, align_bytes=64)
+        w_codes = keep.tile([P, 3, D], U32, align_bytes=64)
+        w_scales = keep.tile([P, 3, D], U8, align_bytes=64)
+        identity = keep.tile([P, P], F32)
+
+        def load_weight(index, w):
+            nc.sync.dma_start(
+                out=w_raw[:, index].rearrange("p (u e) c -> p u (e c)", u=2),
+                in_=w.rearrange("(u p e) c -> p u (e c)", u=2, e=2),
+            )
+
+        def load_group(group):
+            n = group["tiles"]
+            start = group["first_tile"] * D
+            nc.sync.dma_start(
+                out=x_all[:, start : start + n * D],
+                in_=group["rows"].rearrange("(p j) k -> p (j k)", j=n),
+            )
+            if group["loads_tables"]:
+                for table_sb, table in ((cos_sb, cos), (sin_sb, sin)):
+                    nc.sync.dma_start(
+                        out=table_sb[:, group["slot"] : group["slot"] + n, :],
+                        in_=table[group["table_row"] : group["table_row"] + n * P, :].rearrange(
+                            "(p j) d -> p j d", j=n
+                        ),
+                    )
+
+        load_weight(0, wq)
+        load_weight(V, wv)
+        load_weight(1, wk)
+        load_group(groups[0])
+        for group in groups[1:]:
+            load_group(group)
+
+        make_identity(nc, identity[:])
+
+        def transpose_tokens(group):
+            n = group["tiles"]
+            grouped = stage.tile([P, GROUP * P * PACK], BF16, align_bytes=64)
+            grouped_words = grouped[:].bitcast(F32)
+            for i0 in range(0, n, 2):
+                m = min(2, n - i0)
+                xt = psum.tile([P, 2, 2, P], F32)
+                for i in range(m):
+                    for u in range(2):
+                        start = (group["first_tile"] + i0 + i) * WORDS + u * P
+                        nc.tensor.transpose(xt[:, i, u, :], x_words[:, start : start + P], identity[:])
+                nc.scalar.copy(
+                    out=grouped_words[:, i0 * 2 * P : (i0 + m) * 2 * P].rearrange(
+                        "p (i r u) -> p i r u", i=m, u=2
+                    ),
+                    in_=xt[:, 0:m].rearrange("p i u r -> p i r u"),
+                )
+            if group["loads_tables"]:
+                minus = sin_sb[:, group["slot"] : group["slot"] + n, 0:HALF]
+                nc.scalar.mul(out=minus, in_=minus, mul=-1.0)
+            return grouped
+
+        def quantise_tokens(group, grouped):
+            n = group["tiles"]
+            x_codes = stage.tile([P, GROUP * P], U32, align_bytes=64)
+            x_scales = stage.tile([P, GROUP * P], U8, align_bytes=64)
+            nc.vector.quantize_mx(
+                out=x_codes[:, : n * P].bitcast(FP8X4),
+                scales=x_scales[:, : n * P],
+                in_=grouped[:, : n * P * PACK],
+            )
+            return x_codes, x_scales
+
+        def quantise_weights(bank):
+            nc.vector.quantize_mx(
+                out=w_codes[:, bank].bitcast(FP8X4),
+                scales=w_scales[:, bank],
+                in_=w_grouped[:, bank].rearrange("p c t -> p (c t)"),
+            )
+
+        nc.scalar.copy(out=w_grouped[:, V], in_=w_raw[:, V].rearrange("p t c -> p c t"))
+        for qk in range(2):
+            by_half = w_raw[:, qk].rearrange("p t (h s d) -> p s h d t", s=2, d=HALF)
+            for half in (FIRST, SECOND):
+                nc.vector.tensor_copy(
+                    out=w_grouped[:, half, qk * H * HALF : (qk + 1) * H * HALF, :].rearrange(
+                        "p (h d) t -> p h d t", h=H
+                    ),
+                    in_=by_half[:, half],
+                )
+        quantise_weights(FIRST)
+        quantise_weights(SECOND)
+        quantise_weights(V)
+
+        grouped = transpose_tokens(groups[0])
+        x_codes, x_scales = quantise_tokens(groups[0], grouped)
+
+        def heads(bank):
+            return bank[:].rearrange("p (q h d) -> p q h d", q=2, h=H)
+
+        def half_of(product, i, half):
+            return product[:, :, i, :].rearrange("p q (h s d) -> p q h s d", s=2, d=HALF)[:, :, :, half, :]
+
+        def table_half(table_sb, slot, half):
+            one = table_sb[:, slot, half * HALF : (half + 1) * HALF]
+            return one.unsqueeze(1).unsqueeze(1).to_broadcast([P, 2, H, HALF])
+
+        for index, group in enumerate(groups):
+            n = group["tiles"]
+            following = groups[index + 1] if index + 1 < len(groups) else None
+            by_cos = results.tile([P, 2, GROUP, D], F32)
+            by_sin = stage.tile([P, 2, GROUP, D], F32)
+            v_sb = results.tile([P, GROUP, D], F32)
+
+            for i in range(n):
+                columns = slice(i * P, (i + 1) * P)
+                banks = []
+                for bank in (FIRST, SECOND, V):
+                    acc = psum.tile([P, D], F32, name=BANK_TAGS[bank])
+                    nc.tensor.matmul_mx(
+                        out=acc[:],
+                        lhsT=x_codes[:, columns].bitcast(FP8X4),
+                        lhsT_scale=x_scales[:, columns],
+                        rhs=w_codes[:, bank].bitcast(FP8X4),
+                        rhs_scale=w_scales[:, bank],
+                        start=True,
+                        stop=True,
+                    )
+                    banks.append(acc)
+
+                if i == 0 and following is not None:
+                    grouped = transpose_tokens(following)
+
+                slot = group["slot"] + i
+                for bank, cos_half in ((FIRST, 0), (SECOND, 1)):
+                    nc.vector.tensor_tensor(
+                        out=half_of(by_cos, i, cos_half),
+                        in0=heads(banks[bank]),
+                        in1=table_half(cos_sb, slot, cos_half),
+                        op=MULT,
+                    )
+                    nc.vector.tensor_tensor(
+                        out=half_of(by_sin, i, 1 - cos_half),
+                        in0=heads(banks[bank]),
+                        in1=table_half(sin_sb, slot, 1 - cos_half),
+                        op=MULT,
+                    )
+                nc.scalar.copy(out=v_sb[:, i, :], in_=banks[V][:])
+
+                if i == min(1, n - 1) and following is not None:
+                    next_codes, next_scales = quantise_tokens(following, grouped)
+
+                if (i + 1) % ADD_TILES == 0 or i == n - 1:
+                    i0 = i - i % ADD_TILES
+                    nc.gpsimd.tensor_tensor(
+                        out=by_cos[:, :, i0 : i + 1, :],
+                        in0=by_cos[:, :, i0 : i + 1, :],
+                        in1=by_sin[:, :, i0 : i + 1, :],
+                        op=ADD,
+                    )
+
+            for b, row in group["stores"]:
+                for out, result in ((out_2, v_sb[:, 0:n, :]), (out_0, by_cos[:, 0, 0:n, :]), (out_1, by_cos[:, 1, 0:n, :])):
+                    nc.sync.dma_start(
+                        out=out[b, row : row + n * P].rearrange("(p j) h d -> p (j h d)", j=n),
+                        in_=result.rearrange("p j c -> p (j c)"),
+                    )
+
+            if following is not None:
+                x_codes, x_scales = next_codes, next_scales

@@ -35,7 +35,16 @@ FLOPS = 2 * B * (L + P) * D * 3 * D
 
 
 def token_groups(x, pmem):
-    groups = []
+    groups = [
+        {
+            "rows": pmem[0],
+            "tiles": 1,
+            "slot": GROUPS_PER_SEQ * GROUP,
+            "table_row": 0,
+            "loads_tables": True,
+            "stores": [(b, 0) for b in range(B)],
+        }
+    ]
     for b in range(B):
         for g in range(GROUPS_PER_SEQ):
             row = g * GROUP_TOKENS
@@ -49,16 +58,6 @@ def token_groups(x, pmem):
                     "stores": [(b, P + row)],
                 }
             )
-    groups.append(
-        {
-            "rows": pmem[0],
-            "tiles": 1,
-            "slot": GROUPS_PER_SEQ * GROUP,
-            "table_row": 0,
-            "loads_tables": True,
-            "stores": [(b, 0) for b in range(B)],
-        }
-    )
     first_tile = 0
     for group in groups:
         group["first_tile"] = first_tile
@@ -110,9 +109,9 @@ def tile_titanstnt_pa_t_kernel(tc, x, pmem, cos, sin, wq, wk, wv, out_0, out_1, 
                     )
 
         load_weight(0, wq)
-        load_weight(V, wv)
         load_weight(1, wk)
         load_group(groups[0])
+        load_weight(V, wv)
         for group in groups[1:]:
             load_group(group)
 
@@ -158,22 +157,27 @@ def tile_titanstnt_pa_t_kernel(tc, x, pmem, cos, sin, wq, wk, wv, out_0, out_1, 
                 in_=w_grouped[:, bank].rearrange("p c t -> p (c t)"),
             )
 
-        nc.scalar.copy(out=w_grouped[:, V], in_=w_raw[:, V].rearrange("p t c -> p c t"))
-        for qk in range(2):
-            by_half = w_raw[:, qk].rearrange("p t (h s d) -> p s h d t", s=2, d=HALF)
-            for half in (FIRST, SECOND):
-                nc.vector.tensor_copy(
-                    out=w_grouped[:, half, qk * H * HALF : (qk + 1) * H * HALF, :].rearrange(
+        def group_weight(index):
+            by_half = w_raw[:, index].rearrange("p t (h s d) -> p s h d t", s=2, d=HALF)
+            for half, copy in ((FIRST, nc.vector.tensor_copy), (SECOND, nc.scalar.copy)):
+                if index == V:
+                    sorted_columns = w_grouped[:, V].rearrange("p (h s d) t -> p s h d t", s=2, d=HALF)[:, half]
+                else:
+                    sorted_columns = w_grouped[:, half, index * H * HALF : (index + 1) * H * HALF, :].rearrange(
                         "p (h d) t -> p h d t", h=H
-                    ),
-                    in_=by_half[:, half],
-                )
+                    )
+                copy(out=sorted_columns, in_=by_half[:, half])
+
+        group_weight(0)
+        group_weight(1)
         quantise_weights(FIRST)
         quantise_weights(SECOND)
-        quantise_weights(V)
 
         grouped = transpose_tokens(groups[0])
         x_codes, x_scales = quantise_tokens(groups[0], grouped)
+
+        group_weight(V)
+        quantise_weights(V)
 
         def heads(bank):
             return bank[:].rearrange("p (q h d) -> p q h d", q=2, h=H)
@@ -185,6 +189,14 @@ def tile_titanstnt_pa_t_kernel(tc, x, pmem, cos, sin, wq, wk, wv, out_0, out_1, 
             one = table_sb[:, slot, half * HALF : (half + 1) * HALF]
             return one.unsqueeze(1).unsqueeze(1).to_broadcast([P, 2, H, HALF])
 
+        def store(group, out, result, i0, i1):
+            n = group["tiles"]
+            for b, row in group["stores"]:
+                nc.sync.dma_start(
+                    out=out[b, row : row + n * P].rearrange("(p j) h d -> p j (h d)", j=n)[:, i0:i1, :],
+                    in_=result[:, i0:i1, :],
+                )
+
         for index, group in enumerate(groups):
             n = group["tiles"]
             following = groups[index + 1] if index + 1 < len(groups) else None
@@ -192,10 +204,14 @@ def tile_titanstnt_pa_t_kernel(tc, x, pmem, cos, sin, wq, wk, wv, out_0, out_1, 
             by_sin = stage.tile([P, 2, GROUP, D], F32)
             v_sb = results.tile([P, GROUP, D], F32)
 
+            span = ADD_TILES if following is not None else 1
+
             for i in range(n):
                 columns = slice(i * P, (i + 1) * P)
                 banks = []
                 for bank in (FIRST, SECOND, V):
+                    if bank == V and i == 0 and following is not None:
+                        grouped = transpose_tokens(following)
                     acc = psum.tile([P, D], F32, name=BANK_TAGS[bank])
                     nc.tensor.matmul_mx(
                         out=acc[:],
@@ -208,11 +224,10 @@ def tile_titanstnt_pa_t_kernel(tc, x, pmem, cos, sin, wq, wk, wv, out_0, out_1, 
                     )
                     banks.append(acc)
 
-                if i == 0 and following is not None:
-                    grouped = transpose_tokens(following)
-
                 slot = group["slot"] + i
                 for bank, cos_half in ((FIRST, 0), (SECOND, 1)):
+                    if bank == SECOND and i == min(1, n - 1) and following is not None:
+                        next_codes, next_scales = quantise_tokens(following, grouped)
                     nc.vector.tensor_tensor(
                         out=half_of(by_cos, i, cos_half),
                         in0=heads(banks[bank]),
@@ -225,26 +240,22 @@ def tile_titanstnt_pa_t_kernel(tc, x, pmem, cos, sin, wq, wk, wv, out_0, out_1, 
                         in1=table_half(sin_sb, slot, 1 - cos_half),
                         op=MULT,
                     )
+
                 nc.scalar.copy(out=v_sb[:, i, :], in_=banks[V][:])
+                if i == n - 1:
+                    store(group, out_2, v_sb, 0, n)
 
-                if i == min(1, n - 1) and following is not None:
-                    next_codes, next_scales = quantise_tokens(following, grouped)
-
-                if (i + 1) % ADD_TILES == 0 or i == n - 1:
-                    i0 = i - i % ADD_TILES
-                    nc.gpsimd.tensor_tensor(
+                if (i + 1) % span == 0 or i == n - 1:
+                    i0 = i - i % span
+                    adder = nc.vector if following is None and i == n - 1 else nc.gpsimd
+                    adder.tensor_tensor(
                         out=by_cos[:, :, i0 : i + 1, :],
                         in0=by_cos[:, :, i0 : i + 1, :],
                         in1=by_sin[:, :, i0 : i + 1, :],
                         op=ADD,
                     )
-
-            for b, row in group["stores"]:
-                for out, result in ((out_2, v_sb[:, 0:n, :]), (out_0, by_cos[:, 0, 0:n, :]), (out_1, by_cos[:, 1, 0:n, :])):
-                    nc.sync.dma_start(
-                        out=out[b, row : row + n * P].rearrange("(p j) h d -> p (j h d)", j=n),
-                        in_=result.rearrange("p j c -> p (j c)"),
-                    )
+                    store(group, out_0, by_cos[:, 0], i0, i + 1)
+                    store(group, out_1, by_cos[:, 1], i0, i + 1)
 
             if following is not None:
                 x_codes, x_scales = next_codes, next_scales

@@ -254,8 +254,12 @@ def tile_titanstnt_pa_t_kernel(tc, x, pmem, cos, sin, wq, wk, wv, out_0, out_1, 
                         in1=by_sin[:, :, i0 : i + 1, :],
                         op=ADD,
                     )
-                    store(group, out_0, by_cos[:, 0], i0, i + 1)
-                    store(group, out_1, by_cos[:, 1], i0, i + 1)
+                    if following is None:
+                        store(group, out_0, by_cos[:, 0], i0, i + 1)
+                        store(group, out_1, by_cos[:, 1], i0, i + 1)
+                    elif i == n - 1:
+                        store(group, out_0, by_cos[:, 0], 0, n)
+                        store(group, out_1, by_cos[:, 1], 0, n)
 
             if following is not None:
                 x_codes, x_scales = next_codes, next_scales

@@ -204,8 +204,6 @@ def tile_titanstnt_pa_t_kernel(tc, x, pmem, cos, sin, wq, wk, wv, out_0, out_1, 
             by_sin = stage.tile([P, 2, GROUP, D], F32)
             v_sb = results.tile([P, GROUP, D], F32)
 
-            span = ADD_TILES if following is not None else 1
-
             for i in range(n):
                 columns = slice(i * P, (i + 1) * P)
                 banks = []
@@ -226,8 +224,6 @@ def tile_titanstnt_pa_t_kernel(tc, x, pmem, cos, sin, wq, wk, wv, out_0, out_1, 
 
                 slot = group["slot"] + i
                 for bank, cos_half in ((FIRST, 0), (SECOND, 1)):
-                    if bank == SECOND and i == min(1, n - 1) and following is not None:
-                        next_codes, next_scales = quantise_tokens(following, grouped)
                     nc.vector.tensor_tensor(
                         out=half_of(by_cos, i, cos_half),
                         in0=heads(banks[bank]),
@@ -245,21 +241,23 @@ def tile_titanstnt_pa_t_kernel(tc, x, pmem, cos, sin, wq, wk, wv, out_0, out_1, 
                 if i == n - 1:
                     store(group, out_2, v_sb, 0, n)
 
-                if (i + 1) % span == 0 or i == n - 1:
-                    i0 = i - i % span
-                    adder = nc.vector if following is None and i == n - 1 else nc.gpsimd
-                    adder.tensor_tensor(
-                        out=by_cos[:, :, i0 : i + 1, :],
-                        in0=by_cos[:, :, i0 : i + 1, :],
-                        in1=by_sin[:, :, i0 : i + 1, :],
-                        op=ADD,
-                    )
-                    if following is None:
-                        store(group, out_0, by_cos[:, 0], i0, i + 1)
-                        store(group, out_1, by_cos[:, 1], i0, i + 1)
-                    elif i == n - 1:
-                        store(group, out_0, by_cos[:, 0], 0, n)
-                        store(group, out_1, by_cos[:, 1], 0, n)
+                if i == min(ADD_TILES, n) - 1 and following is not None:
+                    next_codes, next_scales = quantise_tokens(following, grouped)
+
+                if (i + 1) % ADD_TILES == 0 or i == n - 1:
+                    i0 = i - i % ADD_TILES
+                    very_last = following is None and i == n - 1
+                    engine = nc.vector if very_last else nc.gpsimd
+                    step = 1 if very_last else i + 1 - i0
+                    for j in range(i0, i + 1, step):
+                        engine.tensor_tensor(
+                            out=by_cos[:, :, j : j + step, :],
+                            in0=by_cos[:, :, j : j + step, :],
+                            in1=by_sin[:, :, j : j + step, :],
+                            op=ADD,
+                        )
+                        store(group, out_0, by_cos[:, 0], j, j + step)
+                        store(group, out_1, by_cos[:, 1], j, j + step)
 
             if following is not None:
                 x_codes, x_scales = next_codes, next_scales

@@ -197,12 +197,22 @@ def tile_titanstnt_pa_t_kernel(tc, x, pmem, cos, sin, wq, wk, wv, out_0, out_1, 
                     in_=result[:, i0:i1, :],
                 )
 
+        def add_and_store(engine, group, by_cos, by_sin, i0, i1):
+            engine.tensor_tensor(
+                out=by_cos[:, :, i0:i1, :], in0=by_cos[:, :, i0:i1, :], in1=by_sin[:, :, i0:i1, :], op=ADD
+            )
+            store(group, out_0, by_cos[:, 0], i0, i1)
+            store(group, out_1, by_cos[:, 1], i0, i1)
+
         for index, group in enumerate(groups):
             n = group["tiles"]
             following = groups[index + 1] if index + 1 < len(groups) else None
             by_cos = results.tile([P, 2, GROUP, D], F32)
             by_sin = stage.tile([P, 2, GROUP, D], F32)
             v_sb = results.tile([P, GROUP, D], F32)
+
+            span = ADD_TILES if following is not None else 1
+            gpsimd_tiles = n if following is not None else n - ADD_TILES
 
             for i in range(n):
                 columns = slice(i * P, (i + 1) * P)
@@ -238,26 +248,18 @@ def tile_titanstnt_pa_t_kernel(tc, x, pmem, cos, sin, wq, wk, wv, out_0, out_1, 
                     )
 
                 nc.scalar.copy(out=v_sb[:, i, :], in_=banks[V][:])
-                if i == n - 1:
-                    store(group, out_2, v_sb, 0, n)
 
                 if i == min(ADD_TILES, n) - 1 and following is not None:
                     next_codes, next_scales = quantise_tokens(following, grouped)
 
-                if (i + 1) % ADD_TILES == 0 or i == n - 1:
-                    i0 = i - i % ADD_TILES
-                    very_last = following is None and i == n - 1
-                    engine = nc.vector if very_last else nc.gpsimd
-                    step = 1 if very_last else i + 1 - i0
-                    for j in range(i0, i + 1, step):
-                        engine.tensor_tensor(
-                            out=by_cos[:, :, j : j + step, :],
-                            in0=by_cos[:, :, j : j + step, :],
-                            in1=by_sin[:, :, j : j + step, :],
-                            op=ADD,
-                        )
-                        store(group, out_0, by_cos[:, 0], j, j + step)
-                        store(group, out_1, by_cos[:, 1], j, j + step)
+                if (i + 1) % span == 0 or i == n - 1:
+                    i0 = i - i % span
+                    store(group, out_2, v_sb, i0, i + 1)
+                    if i0 < gpsimd_tiles:
+                        add_and_store(nc.gpsimd, group, by_cos, by_sin, i0, i + 1)
+
+            for i in range(gpsimd_tiles, n):
+                add_and_store(nc.vector, group, by_cos, by_sin, i, i + 1)
 
             if following is not None:
                 x_codes, x_scales = next_codes, next_scales

@@ -74,7 +74,6 @@ def tile_titanstnt_pa_t_kernel(tc, x, pmem, cos, sin, wq, wk, wv, out_0, out_1, 
         stage = ctx.enter_context(tc.tile_pool(name="stage", bufs=2))
         results = ctx.enter_context(tc.tile_pool(name="results", bufs=3))
         psum = ctx.enter_context(tc.psum_pool(name="psum", bufs=2))
-        ctx.enter_context(tc.manual_schedule())
 
         x_all = keep.tile([P, TOKEN_TILES * D], BF16)
         x_words = x_all[:].bitcast(F32)

from contextlib import ExitStack

import concourse.mybir as mybir
from concourse.masks import make_identity

F32 = mybir.dt.float32
BF16 = mybir.dt.bfloat16
U32 = mybir.dt.uint32
U8 = mybir.dt.uint8
FP8X4 = mybir.dt.float8_e4m3fn_x4
MULT = mybir.AluOpType.mult
ADD = mybir.AluOpType.add

P = 128
PACK = 4
B = 2
L = 2048
D = 512
H = 4
HD = D // H
HALF = HD // 2
GROUP = 4
GROUP_TOKENS = GROUP * P
GROUPS_PER_SEQ = L // GROUP_TOKENS
TABLE_SLOTS = GROUPS_PER_SEQ * GROUP + 1
TOKEN_TILES = B * GROUPS_PER_SEQ * GROUP + 1
WORDS = D // 2
ADD_TILES = 2
FIRST = 0
SECOND = 1
V = 2
BANK_TAGS = ("first", "second", "v")

FLOPS = 2 * B * (L + P) * D * 3 * D


def token_groups(x, pmem):
    groups = [
        {
            "rows": pmem[0],
            "tiles": 1,
            "slot": GROUPS_PER_SEQ * GROUP,
            "table_row": 0,
            "loads_tables": True,
            "stores": [(b, 0) for b in range(B)],
        }
    ]
    for b in range(B):
        for g in range(GROUPS_PER_SEQ):
            row = g * GROUP_TOKENS
            groups.append(
                {
                    "rows": x[b, row : row + GROUP_TOKENS, :],
                    "tiles": GROUP,
                    "slot": g * GROUP,
                    "table_row": P + row,
                    "loads_tables": b == 0,
                    "stores": [(b, P + row)],
                }
            )
    first_tile = 0
    for group in groups:
        group["first_tile"] = first_tile
        first_tile += group["tiles"]
    return groups


def tile_titanstnt_pa_t_kernel(tc, x, pmem, cos, sin, wq, wk, wv, out_0, out_1, out_2):
    nc = tc.nc
    groups = token_groups(x, pmem)

    with ExitStack() as ctx:
        keep = ctx.enter_context(tc.tile_pool(name="keep", bufs=1))
        stage = ctx.enter_context(tc.tile_pool(name="stage", bufs=2))
        results = ctx.enter_context(tc.tile_pool(name="results", bufs=3))
        psum = ctx.enter_context(tc.psum_pool(name="psum", bufs=2))

        x_all = keep.tile([P, TOKEN_TILES * D], BF16)
        x_words = x_all[:].bitcast(F32)
        cos_sb = keep.tile([P, TABLE_SLOTS, HD], BF16)
        sin_sb = keep.tile([P, TABLE_SLOTS, HD], BF16)
        w_raw = keep.tile([P, 3, PACK, D], BF16)
        w_grouped = keep.tile([P, 3, D, PACK], BF16, align_bytes=64)
        w_codes = keep.tile([P, 3, D], U32, align_bytes=64)
        w_scales = keep.tile([P, 3, D], U8, align_bytes=64)
        identity = keep.tile([P, P], F32)

        def load_weight(index, w):
            nc.sync.dma_start(
                out=w_raw[:, index].rearrange("p (u e) c -> p u (e c)", u=2),
                in_=w.rearrange("(u p e) c -> p u (e c)", u=2, e=2),
            )

        def load_group(group):
            n = group["tiles"]
            start = group["first_tile"] * D
            nc.sync.dma_start(
                out=x_all[:, start : start + n * D],
                in_=group["rows"].rearrange("(p j) k -> p (j k)", j=n),
            )
            if group["loads_tables"]:
                for table_sb, table in ((cos_sb, cos), (sin_sb, sin)):
                    nc.sync.dma_start(
                        out=table_sb[:, group["slot"] : group["slot"] + n, :],
                        in_=table[group["table_row"] : group["table_row"] + n * P, :].rearrange(
                            "(p j) d -> p j d", j=n
                        ),
                    )

        load_weight(0, wq)
        load_weight(1, wk)
        load_group(groups[0])
        load_weight(V, wv)
        for group in groups[1:]:
            load_group(group)

        make_identity(nc, identity[:])

        def transpose_tokens(group):
            n = group["tiles"]
            grouped = stage.tile([P, GROUP * P * PACK], BF16, align_bytes=64)
            grouped_words = grouped[:].bitcast(F32)
            for i0 in range(0, n, 2):
                m = min(2, n - i0)
                xt = psum.tile([P, 2, 2, P], F32)
                for i in range(m):
                    for u in range(2):
                        start = (group["first_tile"] + i0 + i) * WORDS + u * P
                        nc.tensor.transpose(xt[:, i, u, :], x_words[:, start : start + P], identity[:])
                nc.scalar.copy(
                    out=grouped_words[:, i0 * 2 * P : (i0 + m) * 2 * P].rearrange(
                        "p (i r u) -> p i r u", i=m, u=2
                    ),
                    in_=xt[:, 0:m].rearrange("p i u r -> p i r u"),
                )
            if group["loads_tables"]:
                minus = sin_sb[:, group["slot"] : group["slot"] + n, 0:HALF]
                nc.scalar.mul(out=minus, in_=minus, mul=-1.0)
            return grouped

        def quantise_tokens(group, grouped):
            n = group["tiles"]
            x_codes = stage.tile([P, GROUP * P], U32, align_bytes=64)
            x_scales = stage.tile([P, GROUP * P], U8, align_bytes=64)
            nc.vector.quantize_mx(
                out=x_codes[:, : n * P].bitcast(FP8X4),
                scales=x_scales[:, : n * P],
                in_=grouped[:, : n * P * PACK],
            )
            return x_codes, x_scales

        def quantise_weights(bank):
            nc.vector.quantize_mx(
                out=w_codes[:, bank].bitcast(FP8X4),
                scales=w_scales[:, bank],
                in_=w_grouped[:, bank].rearrange("p c t -> p (c t)"),
            )

        def group_weight(index):
            by_half = w_raw[:, index].rearrange("p t (h s d) -> p s h d t", s=2, d=HALF)
            for half, copy in ((FIRST, nc.vector.tensor_copy), (SECOND, nc.scalar.copy)):
                if index == V:
                    sorted_columns = w_grouped[:, V].rearrange("p (h s d) t -> p s h d t", s=2, d=HALF)[:, half]
                else:
                    sorted_columns = w_grouped[:, half, index * H * HALF : (index + 1) * H * HALF, :].rearrange(
                        "p (h d) t -> p h d t", h=H
                    )
                copy(out=sorted_columns, in_=by_half[:, half])

        group_weight(0)
        group_weight(1)
        quantise_weights(FIRST)
        quantise_weights(SECOND)

        grouped = transpose_tokens(groups[0])
        x_codes, x_scales = quantise_tokens(groups[0], grouped)

        group_weight(V)
        quantise_weights(V)

        def heads(bank):
            return bank[:].rearrange("p (q h d) -> p q h d", q=2, h=H)

        def half_of(product, i, half):
            return product[:, :, i, :].rearrange("p q (h s d) -> p q h s d", s=2, d=HALF)[:, :, :, half, :]

        def table_half(table_sb, slot, half):
            one = table_sb[:, slot, half * HALF : (half + 1) * HALF]
            return one.unsqueeze(1).unsqueeze(1).to_broadcast([P, 2, H, HALF])

        def store(group, out, result, i0, i1):
            n = group["tiles"]
            for b, row in group["stores"]:
                nc.sync.dma_start(
                    out=out[b, row : row + n * P].rearrange("(p j) h d -> p j (h d)", j=n)[:, i0:i1, :],
                    in_=result[:, i0:i1, :],
                )

        def add_and_store(engine, group, by_cos, by_sin, i0, i1):
            engine.tensor_tensor(
                out=by_cos[:, :, i0:i1, :], in0=by_cos[:, :, i0:i1, :], in1=by_sin[:, :, i0:i1, :], op=ADD
            )
            store(group, out_0, by_cos[:, 0], i0, i1)
            store(group, out_1, by_cos[:, 1], i0, i1)

        for index, group in enumerate(groups):
            n = group["tiles"]
            following = groups[index + 1] if index + 1 < len(groups) else None
            by_cos = results.tile([P, 2, GROUP, D], F32)
            by_sin = stage.tile([P, 2, GROUP, D], F32)
            v_sb = results.tile([P, GROUP, D], F32)

            span = ADD_TILES if following is not None else 1
            gpsimd_tiles = n if following is not None else n - ADD_TILES

            for i in range(n):
                columns = slice(i * P, (i + 1) * P)
                banks = []
                for bank in (FIRST, SECOND, V):
                    if bank == V and i == 0 and following is not None:
                        grouped = transpose_tokens(following)
                    acc = psum.tile([P, D], F32, name=BANK_TAGS[bank])
                    nc.tensor.matmul_mx(
                        out=acc[:],
                        lhsT=x_codes[:, columns].bitcast(FP8X4),
                        lhsT_scale=x_scales[:, columns],
                        rhs=w_codes[:, bank].bitcast(FP8X4),
                        rhs_scale=w_scales[:, bank],
                        start=True,
                        stop=True,
                    )
                    banks.append(acc)

                slot = group["slot"] + i
                for bank, cos_half in ((FIRST, 0), (SECOND, 1)):
                    nc.vector.tensor_tensor(
                        out=half_of(by_cos, i, cos_half),
                        in0=heads(banks[bank]),
                        in1=table_half(cos_sb, slot, cos_half),
                        op=MULT,
                    )
                    nc.vector.tensor_tensor(
                        out=half_of(by_sin, i, 1 - cos_half),
                        in0=heads(banks[bank]),
                        in1=table_half(sin_sb, slot, 1 - cos_half),
                        op=MULT,
                    )

                nc.scalar.copy(out=v_sb[:, i, :], in_=banks[V][:])

                if i == min(ADD_TILES, n) - 1 and following is not None:
                    next_codes, next_scales = quantise_tokens(following, grouped)

                if (i + 1) % span == 0 or i == n - 1:
                    i0 = i - i % span
                    store(group, out_2, v_sb, i0, i + 1)
                    if i0 < gpsimd_tiles:
                        add_and_store(nc.gpsimd, group, by_cos, by_sin, i0, i + 1)

            for i in range(gpsimd_tiles, n):
                add_and_store(nc.vector, group, by_cos, by_sin, i, i + 1)

            if following is not None:
                x_codes, x_scales = next_codes, next_scales
